import numpy as np
import ml_dtypes

BF16 = ml_dtypes.bfloat16


def bf(x):
    return np.asarray(x, np.float32).astype(BF16)


def f32(x):
    return np.asarray(x, np.float32)


def f64(x):
    return np.asarray(x).astype(np.float64)


def striped(idx):
    return np.tile(idx.reshape(-1, 16).T, (8, 1))


S, D, M, K, H, R, N = 256, 128, 256, 4, 128, 8, 1024


def setup_inputs():
    idx = np.concatenate([np.random.permutation(S)[:H] for _ in range(R)])
    return {"table": bf(np.random.standard_normal((S, D))), "wx": bf(np.random.standard_normal((D, M)) / np.sqrt(D)), "bx": f32(0.1 * np.random.standard_normal((M, 1))), "wn": bf(np.random.standard_normal((D, M)) / np.sqrt(D)), "bn": f32(0.1 * np.random.standard_normal((M, 1))), "offs": striped(idx)}


def reference(table, wx, bx, wn, bn, offs):
    idx = offs[:16].T.reshape(-1)
    t = f64(table)
    h_self = f64(wx).T @ t.T + f64(bx)
    proj = f64(wn).T @ t[idx].T
    h_nei = proj.reshape(M, K, S).sum(axis=1) * (1.0 / K) + f64(bn)
    return np.concatenate([h_self, h_nei], axis=0)

@@ -1,0 +1,71 @@
+import concourse.mybir as mybir
+from concourse.masks import make_identity
+
+P = 128
+NODES = 256
+OUT_FEATURES = 256
+NEIGHBOURS = 4
+LIST = NEIGHBOURS * NODES
+PIECE = 128
+PER_COLUMN = 16
+NODE_BLOCKS = NODES // P
+FEATURE_BLOCKS = OUT_FEATURES // P
+
+FLOPS = 2 * P * OUT_FEATURES * (NODES + LIST)
+
+BF16, F32, U16 = mybir.dt.bfloat16, mybir.dt.float32, mybir.dt.uint16
+MULT, ADD = mybir.AluOpType.mult, mybir.AluOpType.add
+IDENTITY = mybir.ActivationFunctionType.Identity
+
+
+def tile_batchedgraphsagemean1_kernel(tc, table, wx, bx, wn, bn, offs, out):
+    nc = tc.nc
+    with (
+        tc.tile_pool(name="held", bufs=1) as held,
+        tc.psum_pool(name="psum", bufs=1) as psum,
+    ):
+        table_rows = held.tile([P, NODE_BLOCKS, P], BF16, name="table_rows")
+        nc.scalar.dma_start(table_rows[:], table.rearrange("(b p) d -> p b d", p=P))
+        offsets = held.tile([P, LIST // PER_COLUMN], U16, name="offsets")
+        nc.sync.dma_start(offsets[:], offs)
+        wx_sb = held.tile([P, OUT_FEATURES], BF16, name="wx_sb")
+        nc.sync.dma_start(wx_sb[:], wx)
+        wn_sb = held.tile([P, OUT_FEATURES], BF16, name="wn_sb")
+        nc.scalar.dma_start(wn_sb[:], wn)
+        bx_sb = held.tile([P, FEATURE_BLOCKS, 1], F32, name="bx_sb")
+        bn_sb = held.tile([P, FEATURE_BLOCKS, 1], F32, name="bn_sb")
+        with nc.allow_non_contiguous_dma(reason="256 biases, one float32 to a partition"):
+            nc.gpsimd.dma_start(bx_sb[:], bx.rearrange("(b p) o -> p b o", p=P))
+            nc.gpsimd.dma_start(bn_sb[:], bn.rearrange("(b p) o -> p b o", p=P))
+
+        identity = held.tile([P, P], BF16, name="identity")
+        make_identity(nc, identity[:])
+        flipped = psum.tile([P, NODES], BF16, name="flipped")
+        for b in range(NODE_BLOCKS):
+            nc.tensor.transpose(flipped[:, b * P : (b + 1) * P], table_rows[:, b, :], identity[:])
+        table_cols = held.tile([P, NODES], BF16, name="table_cols")
+        nc.vector.tensor_copy(table_cols[:], flipped[:])
+
+        for f in range(FEATURE_BLOCKS):
+            own = psum.tile([P, NODES], F32, name=f"own{f}")
+            nc.tensor.matmul(own[:], wx_sb[:, f * P : (f + 1) * P], table_cols[:], start=True, stop=True)
+            own_out = held.tile([P, NODES], F32, name=f"own_out{f}")
+            nc.scalar.activation(own_out[:], own[:], IDENTITY, bias=bx_sb[:, f, :], scale=1.0)
+            nc.sync.dma_start(out[f * P : (f + 1) * P, :], own_out[:])
+
+        for f in range(FEATURE_BLOCKS):
+            mean = psum.tile([P, NODES], F32, name=f"mean{f}")
+            for n0 in range(0, NODES, PIECE):
+                for k in range(NEIGHBOURS):
+                    first = (k * NODES + n0) // PER_COLUMN
+                    piece = offsets[:, first : first + PIECE // PER_COLUMN]
+                    nc.tensor.matmul(
+                        mean[:, n0 : n0 + PIECE],
+                        wn_sb[:, f * P : (f + 1) * P],
+                        table_cols[:].indirect(piece),
+                        start=(k == 0),
+                        stop=(k == NEIGHBOURS - 1),
+                    )
+            mean_out = held.tile([P, NODES], F32, name=f"mean_out{f}")
+            nc.vector.tensor_scalar(mean_out[:], mean[:], 1.0 / NEIGHBOURS, bn_sb[:, f, :], MULT, ADD)
+            nc.scalar.dma_start(out[OUT_FEATURES + f * P : OUT_FEATURES + (f + 1) * P, :], mean_out[:])

@@ -25,18 +25,18 @@ def tile_batchedgraphsagemean1_kernel(tc, table, wx, bx, wn, bn, offs, out):
         tc.psum_pool(name="psum", bufs=1) as psum,
     ):
         table_rows = held.tile([P, NODE_BLOCKS, P], BF16, name="table_rows")
-        nc.scalar.dma_start(table_rows[:], table.rearrange("(b p) d -> p b d", p=P))
+        nc.sync.dma_start(table_rows[:], table.rearrange("(b p) d -> p b d", p=P))
+        wx_sb = held.tile([P, OUT_FEATURES], BF16, name="wx_sb")
+        nc.scalar.dma_start(wx_sb[:], wx)
         offsets = held.tile([P, LIST // PER_COLUMN], U16, name="offsets")
         nc.sync.dma_start(offsets[:], offs)
-        wx_sb = held.tile([P, OUT_FEATURES], BF16, name="wx_sb")
-        nc.sync.dma_start(wx_sb[:], wx)
         wn_sb = held.tile([P, OUT_FEATURES], BF16, name="wn_sb")
         nc.scalar.dma_start(wn_sb[:], wn)
         bx_sb = held.tile([P, FEATURE_BLOCKS, 1], F32, name="bx_sb")
         bn_sb = held.tile([P, FEATURE_BLOCKS, 1], F32, name="bn_sb")
         with nc.allow_non_contiguous_dma(reason="256 biases, one float32 to a partition"):
-            nc.gpsimd.dma_start(bx_sb[:], bx.rearrange("(b p) o -> p b o", p=P))
-            nc.gpsimd.dma_start(bn_sb[:], bn.rearrange("(b p) o -> p b o", p=P))
+            nc.sync.dma_start(bx_sb[:], bx.rearrange("(b p) o -> p b o", p=P))
+            nc.scalar.dma_start(bn_sb[:], bn.rearrange("(b p) o -> p b o", p=P))
 
         identity = held.tile([P, P], BF16, name="identity")
         make_identity(nc, identity[:])

@@ -6,7 +6,7 @@ NODES = 256
 OUT_FEATURES = 256
 NEIGHBOURS = 4
 LIST = NEIGHBOURS * NODES
-PIECE = 128
+PAIR = 2
 PER_COLUMN = 16
 NODE_BLOCKS = NODES // P
 FEATURE_BLOCKS = OUT_FEATURES // P
@@ -54,18 +54,21 @@ def tile_batchedgraphsagemean1_kernel(tc, table, wx, bx, wn, bn, offs, out):
             nc.sync.dma_start(out[f * P : (f + 1) * P, :], own_out[:])
 
         for f in range(FEATURE_BLOCKS):
-            mean = psum.tile([P, NODES], F32, name=f"mean{f}")
-            for n0 in range(0, NODES, PIECE):
-                for k in range(NEIGHBOURS):
-                    first = (k * NODES + n0) // PER_COLUMN
-                    piece = offsets[:, first : first + PIECE // PER_COLUMN]
+            pair_sums = []
+            for k0 in range(0, NEIGHBOURS, PAIR):
+                pair_sum = psum.tile([P, NODES], F32, name=f"pair_sum{f}_{k0}")
+                for k in range(k0, k0 + PAIR):
+                    first = k * NODES // PER_COLUMN
                     nc.tensor.matmul(
-                        mean[:, n0 : n0 + PIECE],
+                        pair_sum[:],
                         wn_sb[:, f * P : (f + 1) * P],
-                        table_cols[:].indirect(piece),
-                        start=(k == 0),
-                        stop=(k == NEIGHBOURS - 1),
+                        table_cols[:].indirect(offsets[:, first : first + NODES // PER_COLUMN]),
+                        start=(k == k0),
+                        stop=(k == k0 + PAIR - 1),
                     )
+                pair_sums.append(pair_sum)
+            first_part = held.tile([P, NODES], F32, name=f"first_part{f}")
+            nc.scalar.activation(first_part[:], pair_sums[0][:], IDENTITY, bias=bn_sb[:, f, :], scale=1.0 / NEIGHBOURS)
             mean_out = held.tile([P, NODES], F32, name=f"mean_out{f}")
-            nc.vector.tensor_scalar(mean_out[:], mean[:], 1.0 / NEIGHBOURS, bn_sb[:, f, :], MULT, ADD)
+            nc.vector.scalar_tensor_tensor(mean_out[:], pair_sums[1][:], 1.0 / NEIGHBOURS, first_part[:], MULT, ADD)
             nc.scalar.dma_start(out[OUT_FEATURES + f * P : OUT_FEATURES + (f + 1) * P, :], mean_out[:])

@@ -27,16 +27,17 @@ def tile_batchedgraphsagemean1_kernel(tc, table, wx, bx, wn, bn, offs, out):
         table_rows = held.tile([P, NODE_BLOCKS, P], BF16, name="table_rows")
         nc.sync.dma_start(table_rows[:], table.rearrange("(b p) d -> p b d", p=P))
         wx_sb = held.tile([P, OUT_FEATURES], BF16, name="wx_sb")
-        nc.scalar.dma_start(wx_sb[:], wx)
-        offsets = held.tile([P, LIST // PER_COLUMN], U16, name="offsets")
-        nc.sync.dma_start(offsets[:], offs)
-        wn_sb = held.tile([P, OUT_FEATURES], BF16, name="wn_sb")
-        nc.scalar.dma_start(wn_sb[:], wn)
+        nc.sync.dma_start(wx_sb[:], wx)
         bx_sb = held.tile([P, FEATURE_BLOCKS, 1], F32, name="bx_sb")
         bn_sb = held.tile([P, FEATURE_BLOCKS, 1], F32, name="bn_sb")
+        offsets = held.tile([P, LIST // PER_COLUMN], U16, name="offsets")
+        wn_sb = held.tile([P, OUT_FEATURES], BF16, name="wn_sb")
         with nc.allow_non_contiguous_dma(reason="256 biases, one float32 to a partition"):
             nc.sync.dma_start(bx_sb[:], bx.rearrange("(b p) o -> p b o", p=P))
-            nc.scalar.dma_start(bn_sb[:], bn.rearrange("(b p) o -> p b o", p=P))
+        nc.sync.dma_start(offsets[:], offs)
+        nc.sync.dma_start(wn_sb[:], wn)
+        with nc.allow_non_contiguous_dma(reason="256 biases, one float32 to a partition"):
+            nc.sync.dma_start(bn_sb[:], bn.rearrange("(b p) o -> p b o", p=P))
 
         identity = held.tile([P, P], BF16, name="identity")
         make_identity(nc, identity[:])

@@ -41,17 +41,25 @@ def tile_batchedgraphsagemean1_kernel(tc, table, wx, bx, wn, bn, offs, out):
 
         identity = held.tile([P, P], BF16, name="identity")
         make_identity(nc, identity[:])
-        flipped = psum.tile([P, NODES], BF16, name="flipped")
-        for b in range(NODE_BLOCKS):
-            nc.tensor.transpose(flipped[:, b * P : (b + 1) * P], table_rows[:, b, :], identity[:])
         table_cols = held.tile([P, NODES], BF16, name="table_cols")
-        nc.vector.tensor_copy(table_cols[:], flipped[:])
+        for b in range(NODE_BLOCKS):
+            flipped = psum.tile([P, P], BF16, name=f"flipped{b}")
+            nc.tensor.transpose(flipped[:], table_rows[:, b, :], identity[:])
+            nc.vector.tensor_copy(table_cols[:, b * P : (b + 1) * P], flipped[:])
 
+        owns = [psum.tile([P, NODES], F32, name=f"own{f}") for f in range(FEATURE_BLOCKS)]
+        for b in range(NODE_BLOCKS):
+            for f in range(FEATURE_BLOCKS):
+                nc.tensor.matmul(
+                    owns[f][:, b * P : (b + 1) * P],
+                    wx_sb[:, f * P : (f + 1) * P],
+                    table_cols[:, b * P : (b + 1) * P],
+                    start=True,
+                    stop=True,
+                )
         for f in range(FEATURE_BLOCKS):
-            own = psum.tile([P, NODES], F32, name=f"own{f}")
-            nc.tensor.matmul(own[:], wx_sb[:, f * P : (f + 1) * P], table_cols[:], start=True, stop=True)
             own_out = held.tile([P, NODES], F32, name=f"own_out{f}")
-            nc.scalar.activation(own_out[:], own[:], IDENTITY, bias=bx_sb[:, f, :], scale=1.0)
+            nc.scalar.activation(own_out[:], owns[f][:], IDENTITY, bias=bx_sb[:, f, :], scale=1.0)
             nc.sync.dma_start(out[f * P : (f + 1) * P, :], own_out[:])
 
         for f in range(FEATURE_BLOCKS):

@@ -80,4 +80,4 @@ def tile_batchedgraphsagemean1_kernel(tc, table, wx, bx, wn, bn, offs, out):
             nc.scalar.activation(first_part[:], pair_sums[0][:], IDENTITY, bias=bn_sb[:, f, :], scale=1.0 / NEIGHBOURS)
             mean_out = held.tile([P, NODES], F32, name=f"mean_out{f}")
             nc.vector.scalar_tensor_tensor(mean_out[:], pair_sums[1][:], 1.0 / NEIGHBOURS, first_part[:], MULT, ADD)
-            nc.scalar.dma_start(out[OUT_FEATURES + f * P : OUT_FEATURES + (f + 1) * P, :], mean_out[:])
+            nc.sync.dma_start(out[OUT_FEATURES + f * P : OUT_FEATURES + (f + 1) * P, :], mean_out[:])

@@ -10,6 +10,9 @@ PAIR = 2
 PER_COLUMN = 16
 NODE_BLOCKS = NODES // P
 FEATURE_BLOCKS = OUT_FEATURES // P
+WARM_COLUMNS = 512
+WARM_MATMULS = 2
+LAST_PAIR_TAG = f"pair_sum{FEATURE_BLOCKS - 1}_{NEIGHBOURS - PAIR}"
 
 FLOPS = 2 * P * OUT_FEATURES * (NODES + LIST)
 
@@ -24,6 +27,12 @@ def tile_batchedgraphsagemean1_kernel(tc, table, wx, bx, wn, bn, offs, out):
         tc.tile_pool(name="held", bufs=1) as held,
         tc.psum_pool(name="psum", bufs=1) as psum,
     ):
+        zeros = held.tile([P, WARM_COLUMNS], BF16, name="zeros")
+        nc.vector.memset(zeros[:], 0.0)
+        unread = psum.tile([P, WARM_COLUMNS], F32, name="unread", tag=LAST_PAIR_TAG)
+        for w in range(WARM_MATMULS):
+            nc.tensor.matmul(unread[:], zeros[:, :P], zeros[:], start=True, stop=True)
+
         table_rows = held.tile([P, NODE_BLOCKS, P], BF16, name="table_rows")
         nc.sync.dma_start(table_rows[:], table.rearrange("(b p) d -> p b d", p=P))
         wx_sb = held.tile([P, OUT_FEATURES], BF16, name="wx_sb")

@@ -27,6 +27,11 @@ def tile_batchedgraphsagemean1_kernel(tc, table, wx, bx, wn, bn, offs, out):
         tc.tile_pool(name="held", bufs=1) as held,
         tc.psum_pool(name="psum", bufs=1) as psum,
     ):
+        spark = held.tile([P, 1], F32, name="spark")
+        nc.vector.memset(spark[:], 0.0)
+        spark_out = held.tile([P, 1], F32, name="spark_out")
+        nc.scalar.activation(spark_out[:], spark[:], IDENTITY)
+
         zeros = held.tile([P, WARM_COLUMNS], BF16, name="zeros")
         nc.vector.memset(zeros[:], 0.0)
         unread = psum.tile([P, WARM_COLUMNS], F32, name="unread", tag=LAST_PAIR_TAG)

@@ -12,7 +12,8 @@ NODE_BLOCKS = NODES // P
 FEATURE_BLOCKS = OUT_FEATURES // P
 WARM_COLUMNS = 512
 WARM_MATMULS = 2
-LAST_PAIR_TAG = f"pair_sum{FEATURE_BLOCKS - 1}_{NEIGHBOURS - PAIR}"
+LAST_PAIR_TAG = "last_pair"
+LAST_RUN = 64
 
 FLOPS = 2 * P * OUT_FEATURES * (NODES + LIST)
 
@@ -77,21 +78,36 @@ def tile_batchedgraphsagemean1_kernel(tc, table, wx, bx, wn, bn, offs, out):
             nc.sync.dma_start(out[f * P : (f + 1) * P, :], own_out[:])
 
         for f in range(FEATURE_BLOCKS):
-            pair_sums = []
-            for k0 in range(0, NEIGHBOURS, PAIR):
-                pair_sum = psum.tile([P, NODES], F32, name=f"pair_sum{f}_{k0}")
-                for k in range(k0, k0 + PAIR):
-                    first = k * NODES // PER_COLUMN
-                    nc.tensor.matmul(
-                        pair_sum[:],
-                        wn_sb[:, f * P : (f + 1) * P],
-                        table_cols[:].indirect(offsets[:, first : first + NODES // PER_COLUMN]),
-                        start=(k == k0),
-                        stop=(k == k0 + PAIR - 1),
-                    )
-                pair_sums.append(pair_sum)
+            wn_block = wn_sb[:, f * P : (f + 1) * P]
+            first_pair = psum.tile([P, NODES], F32, name=f"first_pair{f}")
+            for k in range(PAIR):
+                first = k * NODES // PER_COLUMN
+                nc.tensor.matmul(
+                    first_pair[:],
+                    wn_block,
+                    table_cols[:].indirect(offsets[:, first : first + NODES // PER_COLUMN]),
+                    start=(k == 0),
+                    stop=(k == PAIR - 1),
+                )
             first_part = held.tile([P, NODES], F32, name=f"first_part{f}")
-            nc.scalar.activation(first_part[:], pair_sums[0][:], IDENTITY, bias=bn_sb[:, f, :], scale=1.0 / NEIGHBOURS)
+            nc.scalar.activation(first_part[:], first_pair[:], IDENTITY, bias=bn_sb[:, f, :], scale=1.0 / NEIGHBOURS)
             mean_out = held.tile([P, NODES], F32, name=f"mean_out{f}")
-            nc.vector.scalar_tensor_tensor(mean_out[:], pair_sums[1][:], 1.0 / NEIGHBOURS, first_part[:], MULT, ADD)
+            if f < FEATURE_BLOCKS - 1:
+                runs = [(0, NODES, f"second_pair{f}")]
+            else:
+                runs = [(0, NODES - LAST_RUN, LAST_PAIR_TAG), (NODES - LAST_RUN, NODES, "flipped0")]
+            for lo, hi, tag in runs:
+                second_pair = psum.tile([P, hi - lo], F32, name=f"second_pair{f}_{lo}", tag=tag)
+                for k in range(PAIR, NEIGHBOURS):
+                    first = (k * NODES + lo) // PER_COLUMN
+                    nc.tensor.matmul(
+                        second_pair[:],
+                        wn_block,
+                        table_cols[:].indirect(offsets[:, first : first + (hi - lo) // PER_COLUMN]),
+                        start=(k == PAIR),
+                        stop=(k == NEIGHBOURS - 1),
+                    )
+                nc.vector.scalar_tensor_tensor(
+                    mean_out[:, lo:hi], second_pair[:], 1.0 / NEIGHBOURS, first_part[:, lo:hi], MULT, ADD
+                )
             nc.sync.dma_start(out[OUT_FEATURES + f * P : OUT_FEATURES + (f + 1) * P, :], mean_out[:])

@@ -43,15 +43,14 @@ def tile_batchedgraphsagemean1_kernel(tc, table, wx, bx, wn, bn, offs, out):
         nc.sync.dma_start(table_rows[:], table.rearrange("(b p) d -> p b d", p=P))
         wx_sb = held.tile([P, OUT_FEATURES], BF16, name="wx_sb")
         nc.sync.dma_start(wx_sb[:], wx)
+        offsets = held.tile([P, LIST // PER_COLUMN], U16, name="offsets")
+        nc.sync.dma_start(offsets[:], offs)
+        wn_sb = held.tile([P, OUT_FEATURES], BF16, name="wn_sb")
+        nc.sync.dma_start(wn_sb[:], wn)
         bx_sb = held.tile([P, FEATURE_BLOCKS, 1], F32, name="bx_sb")
         bn_sb = held.tile([P, FEATURE_BLOCKS, 1], F32, name="bn_sb")
-        offsets = held.tile([P, LIST // PER_COLUMN], U16, name="offsets")
-        wn_sb = held.tile([P, OUT_FEATURES], BF16, name="wn_sb")
         with nc.allow_non_contiguous_dma(reason="256 biases, one float32 to a partition"):
             nc.sync.dma_start(bx_sb[:], bx.rearrange("(b p) o -> p b o", p=P))
-        nc.sync.dma_start(offsets[:], offs)
-        nc.sync.dma_start(wn_sb[:], wn)
-        with nc.allow_non_contiguous_dma(reason="256 biases, one float32 to a partition"):
             nc.sync.dma_start(bn_sb[:], bn.rearrange("(b p) o -> p b o", p=P))
 
         identity = held.tile([P, P], BF16, name="identity")

@@ -76,20 +76,23 @@ def tile_batchedgraphsagemean1_kernel(tc, table, wx, bx, wn, bn, offs, out):
             nc.scalar.activation(own_out[:], owns[f][:], IDENTITY, bias=bx_sb[:, f, :], scale=1.0)
             nc.sync.dma_start(out[f * P : (f + 1) * P, :], own_out[:])
 
+        wn_blocks = [wn_sb[:, f * P : (f + 1) * P] for f in range(FEATURE_BLOCKS)]
+        first_parts = []
         for f in range(FEATURE_BLOCKS):
-            wn_block = wn_sb[:, f * P : (f + 1) * P]
             first_pair = psum.tile([P, NODES], F32, name=f"first_pair{f}")
             for k in range(PAIR):
                 first = k * NODES // PER_COLUMN
                 nc.tensor.matmul(
                     first_pair[:],
-                    wn_block,
+                    wn_blocks[f],
                     table_cols[:].indirect(offsets[:, first : first + NODES // PER_COLUMN]),
                     start=(k == 0),
                     stop=(k == PAIR - 1),
                 )
             first_part = held.tile([P, NODES], F32, name=f"first_part{f}")
             nc.scalar.activation(first_part[:], first_pair[:], IDENTITY, bias=bn_sb[:, f, :], scale=1.0 / NEIGHBOURS)
+            first_parts.append(first_part)
+        for f in range(FEATURE_BLOCKS):
             mean_out = held.tile([P, NODES], F32, name=f"mean_out{f}")
             if f < FEATURE_BLOCKS - 1:
                 runs = [(0, NODES, f"second_pair{f}")]
@@ -101,12 +104,12 @@ def tile_batchedgraphsagemean1_kernel(tc, table, wx, bx, wn, bn, offs, out):
                     first = (k * NODES + lo) // PER_COLUMN
                     nc.tensor.matmul(
                         second_pair[:],
-                        wn_block,
+                        wn_blocks[f],
                         table_cols[:].indirect(offsets[:, first : first + (hi - lo) // PER_COLUMN]),
                         start=(k == PAIR),
                         stop=(k == NEIGHBOURS - 1),
                     )
                 nc.vector.scalar_tensor_tensor(
-                    mean_out[:, lo:hi], second_pair[:], 1.0 / NEIGHBOURS, first_part[:, lo:hi], MULT, ADD
+                    mean_out[:, lo:hi], second_pair[:], 1.0 / NEIGHBOURS, first_parts[f][:, lo:hi], MULT, ADD
                 )
             nc.sync.dma_start(out[OUT_FEATURES + f * P : OUT_FEATURES + (f + 1) * P, :], mean_out[:])

@@ -13,7 +13,7 @@ FEATURE_BLOCKS = OUT_FEATURES // P
 WARM_COLUMNS = 512
 WARM_MATMULS = 2
 LAST_PAIR_TAG = "last_pair"
-LAST_RUN = 64
+LAST_RUN = 96
 
 FLOPS = 2 * P * OUT_FEATURES * (NODES + LIST)
 

import concourse.mybir as mybir
from concourse.masks import make_identity

P = 128
NODES = 256
OUT_FEATURES = 256
NEIGHBOURS = 4
LIST = NEIGHBOURS * NODES
PAIR = 2
PER_COLUMN = 16
NODE_BLOCKS = NODES // P
FEATURE_BLOCKS = OUT_FEATURES // P
WARM_COLUMNS = 512
WARM_MATMULS = 2
LAST_PAIR_TAG = "last_pair"
LAST_RUN = 96

FLOPS = 2 * P * OUT_FEATURES * (NODES + LIST)

BF16, F32, U16 = mybir.dt.bfloat16, mybir.dt.float32, mybir.dt.uint16
MULT, ADD = mybir.AluOpType.mult, mybir.AluOpType.add
IDENTITY = mybir.ActivationFunctionType.Identity


def tile_batchedgraphsagemean1_kernel(tc, table, wx, bx, wn, bn, offs, out):
    nc = tc.nc
    with (
        tc.tile_pool(name="held", bufs=1) as held,
        tc.psum_pool(name="psum", bufs=1) as psum,
    ):
        spark = held.tile([P, 1], F32, name="spark")
        nc.vector.memset(spark[:], 0.0)
        spark_out = held.tile([P, 1], F32, name="spark_out")
        nc.scalar.activation(spark_out[:], spark[:], IDENTITY)

        zeros = held.tile([P, WARM_COLUMNS], BF16, name="zeros")
        nc.vector.memset(zeros[:], 0.0)
        unread = psum.tile([P, WARM_COLUMNS], F32, name="unread", tag=LAST_PAIR_TAG)
        for w in range(WARM_MATMULS):
            nc.tensor.matmul(unread[:], zeros[:, :P], zeros[:], start=True, stop=True)

        table_rows = held.tile([P, NODE_BLOCKS, P], BF16, name="table_rows")
        nc.sync.dma_start(table_rows[:], table.rearrange("(b p) d -> p b d", p=P))
        wx_sb = held.tile([P, OUT_FEATURES], BF16, name="wx_sb")
        nc.sync.dma_start(wx_sb[:], wx)
        offsets = held.tile([P, LIST // PER_COLUMN], U16, name="offsets")
        nc.sync.dma_start(offsets[:], offs)
        wn_sb = held.tile([P, OUT_FEATURES], BF16, name="wn_sb")
        nc.sync.dma_start(wn_sb[:], wn)
        bx_sb = held.tile([P, FEATURE_BLOCKS, 1], F32, name="bx_sb")
        bn_sb = held.tile([P, FEATURE_BLOCKS, 1], F32, name="bn_sb")
        with nc.allow_non_contiguous_dma(reason="256 biases, one float32 to a partition"):
            nc.sync.dma_start(bx_sb[:], bx.rearrange("(b p) o -> p b o", p=P))
            nc.sync.dma_start(bn_sb[:], bn.rearrange("(b p) o -> p b o", p=P))

        identity = held.tile([P, P], BF16, name="identity")
        make_identity(nc, identity[:])
        table_cols = held.tile([P, NODES], BF16, name="table_cols")
        for b in range(NODE_BLOCKS):
            flipped = psum.tile([P, P], BF16, name=f"flipped{b}")
            nc.tensor.transpose(flipped[:], table_rows[:, b, :], identity[:])
            nc.vector.tensor_copy(table_cols[:, b * P : (b + 1) * P], flipped[:])

        owns = [psum.tile([P, NODES], F32, name=f"own{f}") for f in range(FEATURE_BLOCKS)]
        for b in range(NODE_BLOCKS):
            for f in range(FEATURE_BLOCKS):
                nc.tensor.matmul(
                    owns[f][:, b * P : (b + 1) * P],
                    wx_sb[:, f * P : (f + 1) * P],
                    table_cols[:, b * P : (b + 1) * P],
                    start=True,
                    stop=True,
                )
        for f in range(FEATURE_BLOCKS):
            own_out = held.tile([P, NODES], F32, name=f"own_out{f}")
            nc.scalar.activation(own_out[:], owns[f][:], IDENTITY, bias=bx_sb[:, f, :], scale=1.0)
            nc.sync.dma_start(out[f * P : (f + 1) * P, :], own_out[:])

        wn_blocks = [wn_sb[:, f * P : (f + 1) * P] for f in range(FEATURE_BLOCKS)]
        first_parts = []
        for f in range(FEATURE_BLOCKS):
            first_pair = psum.tile([P, NODES], F32, name=f"first_pair{f}")
            for k in range(PAIR):
                first = k * NODES // PER_COLUMN
                nc.tensor.matmul(
                    first_pair[:],
                    wn_blocks[f],
                    table_cols[:].indirect(offsets[:, first : first + NODES // PER_COLUMN]),
                    start=(k == 0),
                    stop=(k == PAIR - 1),
                )
            first_part = held.tile([P, NODES], F32, name=f"first_part{f}")
            nc.scalar.activation(first_part[:], first_pair[:], IDENTITY, bias=bn_sb[:, f, :], scale=1.0 / NEIGHBOURS)
            first_parts.append(first_part)
        for f in range(FEATURE_BLOCKS):
            mean_out = held.tile([P, NODES], F32, name=f"mean_out{f}")
            if f < FEATURE_BLOCKS - 1:
                runs = [(0, NODES, f"second_pair{f}")]
            else:
                runs = [(0, NODES - LAST_RUN, LAST_PAIR_TAG), (NODES - LAST_RUN, NODES, "flipped0")]
            for lo, hi, tag in runs:
                second_pair = psum.tile([P, hi - lo], F32, name=f"second_pair{f}_{lo}", tag=tag)
                for k in range(PAIR, NEIGHBOURS):
                    first = (k * NODES + lo) // PER_COLUMN
                    nc.tensor.matmul(
                        second_pair[:],
                        wn_blocks[f],
                        table_cols[:].indirect(offsets[:, first : first + (hi - lo) // PER_COLUMN]),
                        start=(k == PAIR),
                        stop=(k == NEIGHBOURS - 1),
                    )
                nc.vector.scalar_tensor_tensor(
                    mean_out[:, lo:hi], second_pair[:], 1.0 / NEIGHBOURS, first_parts[f][:, lo:hi], MULT, ADD
                )
            nc.sync.dma_start(out[OUT_FEATURES + f * P : OUT_FEATURES + (f + 1) * P, :], mean_out[:])
